import numpy as np
import ml_dtypes


def mxq(x, axis, fmt="e4m3"):
    dtype, down = {"e4m3": (ml_dtypes.float8_e4m3fn, 7), "e5m2": (ml_dtypes.float8_e5m2, 14)}[fmt]
    v = np.moveaxis(np.asarray(x, np.float32).astype(ml_dtypes.bfloat16).astype(np.float64), axis, -1)
    blocks = v.reshape(v.shape[:-1] + (-1, 32))
    amax = np.abs(blocks).max(-1, keepdims=True)
    byte = np.maximum(np.where(amax > 0, np.frexp(amax)[1] - 1 + 127, 0) - down, 1)
    scale = np.exp2(byte - 127.0)
    codes = (blocks / scale).astype(np.float32).astype(dtype).astype(np.float64)
    return np.moveaxis((codes * scale).reshape(v.shape), -1, axis)


WIDE = False


def mx_kscale(k):
    if not WIDE:
        return np.ones(k)
    levels = np.array([10, -10, 5, -5, 0])
    a = np.random.permutation(np.resize(levels, k // 512 * 4)).reshape(k // 512, 4)
    idx = np.arange(k)
    return np.exp2(a[idx // 512, idx % 128 // 32])


BF16 = ml_dtypes.bfloat16


def bf(x):
    return np.asarray(x, np.float32).astype(BF16)


def f64(x):
    return np.asarray(x).astype(np.float64)


E2M1 = np.array([0.0, 0.5, 1.0, 1.5, 2.0, 3.0, 4.0, 6.0, -0.0, -0.5, -1.0, -1.5, -2.0, -3.0, -4.0, -6.0])


def pack_weight(w, fmt):
    k, n = w.shape
    w = f64(bf(w)).reshape(k // 32, 32, n)
    amax = np.abs(w).max(1)
    if fmt == "e4m3":
        byte = np.frexp(amax)[1] - 1 + 127 - 7
    else:
        mant, ex = np.frexp(amax / 6.0)
        byte = np.where(mant > 0.5, ex, ex - 1) + 127
    byte = np.clip(np.where(amax > 0, byte, 1), 1, 254)
    scaled = (w * np.exp2(127.0 - byte)[:, None, :]).reshape(k, n).astype(np.float32)
    by_word = np.ascontiguousarray(scaled.reshape(k // 512, 128, 4, n).transpose(0, 1, 3, 2))
    if fmt == "e4m3":
        words = by_word.astype(ml_dtypes.float8_e4m3fn).view(np.uint8)
    else:
        c = by_word.astype(ml_dtypes.float4_e2m1fn).view(np.uint8) & 0xF
        words = c[..., 0::2] | (c[..., 1::2] << 4)
    return np.ascontiguousarray(words), np.ascontiguousarray(byte.astype(np.uint8).reshape(k // 512, 16, n))


def unpack_weight(words, scales, fmt):
    g, p, n, _ = words.shape
    if fmt == "e4m3":
        vals = np.ascontiguousarray(words).view(ml_dtypes.float8_e4m3fn).astype(np.float64)
    else:
        nib = np.empty((g, p, n, 4), np.uint8)
        nib[..., 0::2] = words & 0xF
        nib[..., 1::2] = words >> 4
        vals = E2M1[nib]
    vals = vals * np.repeat(np.exp2(scales.astype(np.float64) - 127.0), 8, axis=1)[..., None]
    return vals.transpose(0, 1, 3, 2).reshape(g * 512, n)


B, C, O, H, W, KT = 2, 4096, 4096, 8, 8, 7

OFFSETS = ((0, 0), (-1, 0), (1, 0), (0, -1), (0, 1))


def setup_inputs():
    s = mx_kscale(C)
    x = bf(np.random.standard_normal((B, C, H, W)) * s[None, :, None, None])
    w = bf(np.random.standard_normal((len(OFFSETS), C, KT, KT)) * 2.0 / s[None, :, None, None])
    conv_w = np.random.standard_normal((O, C)) / np.sqrt(C) / s[None, :]
    conv_w_words, conv_w_scales = pack_weight(np.ascontiguousarray(conv_w.T), "e4m3")
    conv_b = bf(np.random.standard_normal(O) * 0.3)
    return {"x": x,
            "w": w,
            "conv_w_words": conv_w_words,
            "conv_w_scales": conv_w_scales,
            "conv_b": conv_b}


def reference(x, w, conv_w_words, conv_w_scales, conv_b):
    x, w, conv_b = f64(x), f64(w), f64(conv_b)
    conv_w = unpack_weight(conv_w_words, conv_w_scales, "e4m3").T
    nb_, nc_, hh, ww = x.shape
    k = w.shape[-1]
    ph = k - hh % k
    pw = k - ww % k
    xpd = np.pad(x, ((0, 0), (0, 0), (0, ph), (0, pw)))
    hp, wp = hh + ph, ww + pw
    wpos = np.tile(w, (1, 1, hp // k, wp // k))
    xh = np.pad(xpd, ((0, 0), (0, 0), (1, 1), (1, 1)))
    att = np.zeros_like(xpd)
    for n, (dh, dw) in enumerate(OFFSETS):
        nb = xh[:, :, 1 + dh:1 + dh + hp, 1 + dw:1 + dw + wp]
        att = att + wpos[n][None] * nb
    e = np.exp(att - att.max(axis=1, keepdims=True))
    att = e / e.sum(axis=1, keepdims=True)
    x1 = xpd * att + xpd
    x1 = x1[:, :, :hh, :ww]
    y = np.matmul(conv_w, mxq(x1, 1, "e4m3").reshape(nb_, nc_, hh * ww))
    return y.reshape(nb_, -1, hh, ww) + conv_b[None, :, None, None]

@@ -1,0 +1,340 @@
+from contextlib import ExitStack
+
+from concourse import mybir
+from concourse.masks import make_identity
+
+F32 = mybir.dt.float32
+BF16 = mybir.dt.bfloat16
+I32 = mybir.dt.int32
+U32 = mybir.dt.uint32
+U8 = mybir.dt.uint8
+FP8X4 = mybir.dt.float8_e4m3fn_x4
+ALU = mybir.AluOpType
+ACT = mybir.ActivationFunctionType
+AX = mybir.AxisListType
+
+P = 128
+G = 8
+T = 4
+NB = 2
+NTAP = 5
+O = 4096
+OFFSETS = ((0, 0), (-1, 0), (1, 0), (0, -1), (0, 1))
+W_PITCH = 208
+NPROD = 3
+
+FLOPS = 2 * 128 * 4096 * 4096
+
+N_VEC = 4
+USE_WPS = True
+WAVE = 4
+E_AHEAD = 4
+W_AHEAD = 3
+LOADS = ((0, 2048, 2), (2048, 3072, 4), (3072, 3584, 8), (3584, 4096, 8))
+
+
+def tile_lablock_w_kernel(tc, x, w, conv_w_words, conv_w_scales, conv_b, out):
+    nc = tc.nc
+    with ExitStack() as ctx:
+        keep = ctx.enter_context(tc.tile_pool(name="keep", bufs=1))
+        work = ctx.enter_context(tc.tile_pool(name="work", bufs=3))
+        psum = ctx.enter_context(tc.psum_pool(name="psum", bufs=4))
+        ctx.enter_context(tc.manual_schedule())
+
+        w_words = keep.tile([P, G, O], U32, name="w_words", align_bytes=64)
+        planes = [keep.tile([P, O], U8, name="planes%d" % h, align_bytes=64) for h in range(2)]
+        x_sb = keep.tile([P, NB, G * T, 64], BF16, name="x_sb")
+        w_raw = keep.tile([P, G, NTAP, W_PITCH], BF16, name="w_raw")
+        prods = [keep.tile([P, NTAP, T, NB, 64], F32, name="prod%d" % k) for k in range(NPROD)]
+        e_sb = keep.tile([P, G, 512], F32, name="e_sb")
+        x1_codes = keep.tile([P, G, P], U32, name="x1_codes", align_bytes=64)
+        x1_planes = keep.tile([P, G, P], U8, name="x1_planes", align_bytes=64)
+        ident_f = keep.tile([P, P], F32, name="ident_f")
+        ident_b = keep.tile([P, P], BF16, name="ident_b")
+        bias_rows = keep.tile([P, P], BF16, name="bias_rows")
+        bias_sb = keep.tile([P, 32], F32, name="bias_sb")
+        neg_max = keep.tile([P, G], F32, name="neg_max")
+        part_sum = keep.tile([P, G], F32, name="part_sum")
+        neg_max_all = keep.tile([P, 1], F32, name="neg_max_all")
+        factor = keep.tile([P, G], F32, name="factor")
+        weighted = keep.tile([P, G], F32, name="weighted")
+        total = keep.tile([P, 1], F32, name="total")
+        recip = keep.tile([P, 1], F32, name="recip")
+        coef = keep.tile([P, G], F32, name="coef")
+        warm = keep.tile([P, 1], F32, name="warm")
+
+        def tap_engine(n):
+            return nc.vector if n < N_VEC else nc.gpsimd
+
+        nc.gpsimd.memset(bias_rows[:], 0.0)
+        nc.scalar.dma_start(out=bias_rows[0:32, :], in_=conv_b.rearrange("(k p) -> k p", p=P))
+        nc.vector.memset(warm[:], 0.0)
+        nc.scalar.activation(out=warm[:], in_=warm[:], func=ACT.Exp)
+        make_identity(nc, ident_b[:])
+        make_identity(nc, ident_f[:])
+        for k in range(NPROD):
+            tap_engine(1).memset(prods[k][:, 1, :, :, 0:7], 0.0)
+            tap_engine(1).memset(prods[k][:, 1, :, :, 56:57], 0.0)
+            tap_engine(2).memset(prods[k][:, 2, :, :, 49:56], 0.0)
+            tap_engine(2).memset(prods[k][:, 2, :, :, 63:64], 0.0)
+            tap_engine(3).memset(prods[k][:, 3, :, :, 0:56:7], 0.0)
+            tap_engine(4).memset(prods[k][:, 4, :, :, 56:64], 0.0)
+        for h in range(2):
+            nc.vector.memset(planes[h][:].bitcast(I32), 0)
+
+        x_v = x.rearrange("b (g p t) i j -> g p b (t i j)", g=G, p=P, t=T)
+        w_v = w.rearrange("n (g p t) r s -> g p n (t r s)", g=G, p=P, t=T)
+        for g in range(G):
+            nc.sync.dma_start(out=w_raw[:, g, :, 0:196], in_=w_v[g])
+            nc.sync.dma_start(
+                out=x_sb[:, :, T * g : T * (g + 1), :].rearrange("p b t s -> p b (t s)"), in_=x_v[g]
+            )
+        for h in range(2):
+            for q in range(4):
+                nc.sync.dma_start(
+                    out=planes[h][32 * q : 32 * q + 16, :].bitcast(I32),
+                    in_=conv_w_scales[4 * h : 4 * h + 4, 4 * q : 4 * q + 4, :].bitcast(I32),
+                )
+        words_v = conv_w_words.rearrange("g p n t -> p g (n t)")
+        for n0, n1, gstep in LOADS:
+            for g0 in range(0, G, gstep):
+                nc.sync.dma_start(
+                    out=w_words[:, g0 : g0 + gstep, n0:n1].bitcast(I32),
+                    in_=words_v[:, g0 : g0 + gstep, 4 * n0 : 4 * n1].bitcast(I32),
+                )
+
+        x5 = x_sb[:].rearrange("p b q (i j) -> p b q i j", j=8)
+        w_exps = {}
+        w_pss = {}
+        a_ts = {}
+
+        def raw_w(g):
+            return w_raw[:, g, :, 0:196].rearrange("p n (t k) -> p n t k", k=49)
+
+        def expand(g):
+            w_exp = work.tile([P, N_VEC, T, 64], BF16, name="w_exp", bufs=E_AHEAD + 1)
+            w_exps[g] = w_exp
+            w4 = raw_w(g)[:, 0:N_VEC]
+            nc.scalar.copy(out=w_exp[:, :, :, 0:49], in_=w4)
+            nc.scalar.copy(out=w_exp[:, :, :, 49:56], in_=w4[:, :, :, 0:7])
+            nc.scalar.copy(out=w_exp[:, :, :, 56:63], in_=w4[:, :, :, 0:49:7])
+            nc.scalar.copy(out=w_exp[:, :, :, 63:64], in_=w4[:, :, :, 0:1])
+
+        def stage_w(g):
+            w_ps = psum.tile([P, N_VEC, T, 64], BF16, name="w_ps", tag="acc")
+            w_pss[g] = w_ps
+            for n0 in range(0, N_VEC, 2):
+                n1 = min(N_VEC, n0 + 2)
+                nc.tensor.matmul(
+                    out=w_ps[:, n0:n1].rearrange("p n t s -> p (n t s)"),
+                    lhsT=ident_b[:],
+                    rhs=w_exps[g][:, n0:n1].rearrange("p n t s -> p (n t s)"),
+                    start=True,
+                    stop=True,
+                )
+
+        def products_vector(g, t0, t1):
+            prod = prods[g % NPROD]
+            qs = slice(T * g + t0, T * g + t1)
+            wt = w_pss[g] if USE_WPS else w_exps[g]
+            for n in range(N_VEC):
+                di, dj = OFFSETS[n]
+                ia, ib = max(0, -di), 8 - max(0, di)
+                ja, jb = max(0, -dj), 7
+                for b in range(NB):
+                    nc.vector.tensor_tensor(
+                        out=prod[:, n, t0:t1, b, 0:56].rearrange("p t (i j) -> p t i j", j=7)[:, :, ia:ib, ja:jb],
+                        in0=x5[:, b, qs, ia + di : ib + di, ja + dj : jb + dj],
+                        in1=wt[:, n, t0:t1, 0:56].rearrange("p t (i j) -> p t i j", j=7)[:, :, ia:ib, ja:jb],
+                        op=ALU.mult,
+                    )
+                if dj <= 0:
+                    nc.vector.tensor_tensor(
+                        out=prod[:, n, t0:t1, :, 56 + ia : 56 + ib],
+                        in0=x5[:, :, qs, ia + di : ib + di, 7 + dj].rearrange("p b t i -> p t b i"),
+                        in1=wt[:, n, t0:t1, 56 + ia : 56 + ib].unsqueeze(2).to_broadcast([P, t1 - t0, NB, ib - ia]),
+                        op=ALU.mult,
+                    )
+
+        def products_gpsimd(g, t0, t1):
+            prod = prods[g % NPROD]
+            qs = slice(T * g + t0, T * g + t1)
+            for n in range(N_VEC, NTAP):
+                di, dj = OFFSETS[n]
+                assert di == 0
+                ja, jb = max(0, -dj), 7
+                w4 = raw_w(g)[:, n, t0:t1]
+                for b in range(NB):
+                    nc.gpsimd.tensor_tensor(
+                        out=prod[:, n, t0:t1, b, 0:49].rearrange("p t (i j) -> p t i j", j=7)[:, :, :, ja:jb],
+                        in0=x5[:, b, qs, 0:7, ja + dj : jb + dj],
+                        in1=w4.rearrange("p t (i j) -> p t i j", j=7)[:, :, :, ja:jb],
+                        op=ALU.mult,
+                    )
+                nc.gpsimd.tensor_tensor(
+                    out=prod[:, n, t0:t1, :, 49 + ja : 49 + jb],
+                    in0=x5[:, :, qs, 7, ja + dj : jb + dj].rearrange("p b t j -> p t b j"),
+                    in1=w4[:, :, ja:jb].unsqueeze(2).to_broadcast([P, t1 - t0, NB, jb - ja]),
+                    op=ALU.mult,
+                )
+                if dj <= 0:
+                    nc.gpsimd.tensor_tensor(
+                        out=prod[:, n, t0:t1, :, 56:63],
+                        in0=x5[:, :, qs, 0:7, 7 + dj].rearrange("p b t i -> p t b i"),
+                        in1=w4[:, :, 0:49:7].unsqueeze(2).to_broadcast([P, t1 - t0, NB, 7]),
+                        op=ALU.mult,
+                    )
+                    nc.gpsimd.tensor_tensor(
+                        out=prod[:, n, t0:t1, :, 63:64],
+                        in0=x5[:, :, qs, 7:8, 7 + dj].rearrange("p b t i -> p t b i"),
+                        in1=w4[:, :, 0:1].unsqueeze(2).to_broadcast([P, t1 - t0, NB, 1]),
+                        op=ALU.mult,
+                    )
+
+        def add_taps(g, t0, t1):
+            if t0 == 0:
+                a_ts[g] = psum.tile([P, 512], F32, name="a_t", tag="tp")
+            for t in range(t0, t1):
+                for n in range(NTAP):
+                    nc.tensor.matmul(
+                        out=a_ts[g][:, P * t : P * (t + 1)],
+                        lhsT=prods[g % NPROD][:, n, t].rearrange("p b s -> p (b s)"),
+                        rhs=ident_f[:],
+                        is_transpose=True,
+                        start=(n == 0),
+                        stop=(n == NTAP - 1),
+                    )
+
+        def soft(g):
+            nc.vector.tensor_reduce(out=neg_max[:, g : g + 1], in_=a_ts[g][:], axis=AX.X, op=ALU.max, negate=True)
+            nc.scalar.activation(
+                out=e_sb[:, g, :],
+                in_=a_ts[g][:],
+                func=ACT.Exp,
+                bias=neg_max[:, g : g + 1],
+                scale=1.0,
+                accum_out=part_sum[:, g : g + 1],
+            )
+
+        for g in range(E_AHEAD):
+            expand(g)
+        if USE_WPS:
+            for g in range(W_AHEAD):
+                stage_w(g)
+        for g in range(G):
+            halves = ((0, T),) if g < G - 1 else ((0, 2), (2, T))
+            for t0, t1 in halves:
+                products_gpsimd(g, t0, t1)
+                products_vector(g, t0, t1)
+                add_taps(g, t0, t1)
+            if USE_WPS and g + W_AHEAD < G:
+                stage_w(g + W_AHEAD)
+            if g >= 1:
+                soft(g - 1)
+            if g == 2:
+                bias_ps = psum.tile([P, P], BF16, name="bias_ps", tag="acc")
+                nc.tensor.transpose(bias_ps[:], bias_rows[:], ident_b[:])
+            if g == 4:
+                nc.vector.tensor_copy(out=bias_sb[:], in_=bias_ps[:, 0:32])
+            if g + E_AHEAD < G:
+                expand(g + E_AHEAD)
+        soft(G - 1)
+
+        nc.vector.tensor_reduce(out=neg_max_all[:], in_=neg_max[:], axis=AX.X, op=ALU.min)
+        nc.scalar.activation(out=factor[:], in_=neg_max[:], func=ACT.Exp, bias=neg_max_all[:], scale=-1.0)
+        nc.vector.tensor_tensor(out=weighted[:], in0=factor[:], in1=part_sum[:], op=ALU.mult)
+        nc.vector.tensor_reduce(out=total[:], in_=weighted[:], axis=AX.X, op=ALU.add)
+        nc.vector.reciprocal(out=recip[:], in_=total[:])
+        nc.vector.tensor_scalar(out=coef[:], in0=factor[:], scalar1=recip[:], scalar2=None, op0=ALU.mult)
+
+        u_ts = {}
+        accs = {}
+
+        def back(g):
+            u = work.tile([P, 512], F32, name="u", tag="f32row", bufs=4)
+            nc.scalar.activation(out=u[:], in_=e_sb[:, g, :], func=ACT.Copy, scale=coef[:, g : g + 1], bias=1.0)
+            u_t = psum.tile([P, T, NB, 64], F32, name="u_t", tag="tp")
+            u_ts[g] = u_t
+            for t in range(T):
+                nc.tensor.transpose(
+                    u_t[:, t].rearrange("p b s -> p (b s)"), u[:, P * t : P * (t + 1)], ident_f[:]
+                )
+
+        def quantise(g):
+            qs = slice(T * g, T * (g + 1))
+            u_t = u_ts[g]
+            grouped = work.tile([P, NB, 8, 8, T], BF16, name="grouped", align_bytes=64)
+            for b in range(NB):
+                nc.vector.tensor_tensor(
+                    out=grouped[:, b, :, 0:7, :],
+                    in0=u_t[:, :, b, 0:56].rearrange("p t (i j) -> p i j t", j=7),
+                    in1=x5[:, b, qs, :, 0:7].rearrange("p t i j -> p i j t"),
+                    op=ALU.mult,
+                )
+                nc.vector.tensor_tensor(
+                    out=grouped[:, b, :, 7, :],
+                    in0=u_t[:, :, b, 56:64].rearrange("p t i -> p i t"),
+                    in1=x5[:, b, qs, :, 7].rearrange("p t i -> p i t"),
+                    op=ALU.mult,
+                )
+            nc.vector.quantize_mx(
+                out=x1_codes[:, g, :].bitcast(FP8X4),
+                scales=x1_planes[:, g, :],
+                in_=grouped[:].rearrange("p b i j t -> p (b i j t)"),
+            )
+
+        def mx_pass(bank, k, g):
+            cols = slice(P * (4 * bank + k), P * (4 * bank + k + 1))
+            nc.tensor.matmul_mx(
+                out=accs[bank][:, k, :],
+                lhsT=w_words[:, g, cols].bitcast(FP8X4),
+                lhsT_scale=planes[g // 4][4 * (g % 4) : P, cols],
+                rhs=x1_codes[:, g, :].bitcast(FP8X4),
+                rhs_scale=x1_planes[:, g, :],
+                start=(g == 0),
+                stop=(g == G - 1),
+            )
+
+        def wave(g):
+            for bank in range(WAVE):
+                mx_pass(bank, 0, g)
+
+        for bank in range(WAVE):
+            accs[bank] = psum.tile([P, 4, P], F32, name="acc", tag="acc")
+        for g in range(4):
+            back(g)
+        for pair in range(4):
+            quantise(2 * pair)
+            quantise(2 * pair + 1)
+            if 2 * pair + 4 < G:
+                back(2 * pair + 4)
+                back(2 * pair + 5)
+            wave(2 * pair)
+            wave(2 * pair + 1)
+
+        out_v = out.rearrange("b (k p) i j -> b p k (i j)", p=P)
+        for bank in range(8):
+            if bank >= WAVE:
+                accs[bank] = psum.tile([P, 4, P], F32, name="acc", tag="acc")
+            for k in range(1 if bank < WAVE else 0, 4):
+                for g in range(G):
+                    mx_pass(bank, k, g)
+            acc = accs[bank]
+            res = work.tile([P, 4, NB, 64], F32, name="res", tag="f32row", bufs=4)
+            if bank % 2 == 0:
+                nc.vector.tensor_tensor(
+                    out=res[:].rearrange("p k b s -> p k (b s)"),
+                    in0=acc[:],
+                    in1=bias_sb[:, 4 * bank : 4 * bank + 4].unsqueeze(2).to_broadcast([P, 4, P]),
+                    op=ALU.add,
+                )
+            else:
+                for k in range(4):
+                    nc.scalar.activation(
+                        out=res[:, k].rearrange("p b s -> p (b s)"),
+                        in_=acc[:, k, :],
+                        func=ACT.Identity,
+                        bias=bias_sb[:, 4 * bank + k : 4 * bank + k + 1],
+                    )
+            for b in range(NB):
+                nc.sync.dma_start(out=out_v[b][:, 4 * bank : 4 * bank + 4, :], in_=res[:, :, b, :])

@@ -19,14 +19,12 @@ T = 4
 NB = 2
 NTAP = 5
 O = 4096
-OFFSETS = ((0, 0), (-1, 0), (1, 0), (0, -1), (0, 1))
 W_PITCH = 208
 NPROD = 3
 
 FLOPS = 2 * 128 * 4096 * 4096
 
 N_VEC = 4
-USE_WPS = True
 WAVE = 4
 E_AHEAD = 4
 W_AHEAD = 3
@@ -63,9 +61,6 @@ def tile_lablock_w_kernel(tc, x, w, conv_w_words, conv_w_scales, conv_b, out):
         coef = keep.tile([P, G], F32, name="coef")
         warm = keep.tile([P, 1], F32, name="warm")
 
-        def tap_engine(n):
-            return nc.vector if n < N_VEC else nc.gpsimd
-
         nc.gpsimd.memset(bias_rows[:], 0.0)
         nc.scalar.dma_start(out=bias_rows[0:32, :], in_=conv_b.rearrange("(k p) -> k p", p=P))
         nc.vector.memset(warm[:], 0.0)
@@ -73,12 +68,10 @@ def tile_lablock_w_kernel(tc, x, w, conv_w_words, conv_w_scales, conv_b, out):
         make_identity(nc, ident_b[:])
         make_identity(nc, ident_f[:])
         for k in range(NPROD):
-            tap_engine(1).memset(prods[k][:, 1, :, :, 0:7], 0.0)
-            tap_engine(1).memset(prods[k][:, 1, :, :, 56:57], 0.0)
-            tap_engine(2).memset(prods[k][:, 2, :, :, 49:56], 0.0)
-            tap_engine(2).memset(prods[k][:, 2, :, :, 63:64], 0.0)
-            tap_engine(3).memset(prods[k][:, 3, :, :, 0:56:7], 0.0)
-            tap_engine(4).memset(prods[k][:, 4, :, :, 56:64], 0.0)
+            nc.vector.memset(prods[k][:, 1, :, :, 0:8], 0.0)
+            nc.vector.memset(prods[k][:, 2, :, :, 56:64], 0.0)
+            nc.vector.memset(prods[k][:, 3, :, :, 0:64:8], 0.0)
+            nc.gpsimd.memset(prods[k][:, 4, :, :, 7:64:8], 0.0)
         for h in range(2):
             nc.vector.memset(planes[h][:].bitcast(I32), 0)
 
@@ -109,87 +102,66 @@ def tile_lablock_w_kernel(tc, x, w, conv_w_words, conv_w_scales, conv_b, out):
         a_ts = {}
 
         def raw_w(g):
-            return w_raw[:, g, :, 0:196].rearrange("p n (t k) -> p n t k", k=49)
+            return w_raw[:, g, :, 0:196].rearrange("p n (t i j) -> p n t i j", t=T, i=7)
 
         def expand(g):
-            w_exp = work.tile([P, N_VEC, T, 64], BF16, name="w_exp", bufs=E_AHEAD + 1)
+            w_exp = work.tile([P, N_VEC, T, 8, 8], BF16, name="w_exp", bufs=E_AHEAD + 1)
             w_exps[g] = w_exp
             w4 = raw_w(g)[:, 0:N_VEC]
-            nc.scalar.copy(out=w_exp[:, :, :, 0:49], in_=w4)
-            nc.scalar.copy(out=w_exp[:, :, :, 49:56], in_=w4[:, :, :, 0:7])
-            nc.scalar.copy(out=w_exp[:, :, :, 56:63], in_=w4[:, :, :, 0:49:7])
-            nc.scalar.copy(out=w_exp[:, :, :, 63:64], in_=w4[:, :, :, 0:1])
+            nc.scalar.copy(out=w_exp[:, :, :, 0:7, 0:7], in_=w4)
+            nc.scalar.copy(out=w_exp[:, :, :, 7, 0:7], in_=w4[:, :, :, 0, :])
+            nc.scalar.copy(out=w_exp[:, :, :, 0:7, 7], in_=w4[:, :, :, :, 0])
+            nc.scalar.copy(out=w_exp[:, :, :, 7, 7], in_=w4[:, :, :, 0, 0])
 
         def stage_w(g):
             w_ps = psum.tile([P, N_VEC, T, 64], BF16, name="w_ps", tag="acc")
             w_pss[g] = w_ps
             for n0 in range(0, N_VEC, 2):
-                n1 = min(N_VEC, n0 + 2)
                 nc.tensor.matmul(
-                    out=w_ps[:, n0:n1].rearrange("p n t s -> p (n t s)"),
+                    out=w_ps[:, n0 : n0 + 2].rearrange("p n t s -> p (n t s)"),
                     lhsT=ident_b[:],
-                    rhs=w_exps[g][:, n0:n1].rearrange("p n t s -> p (n t s)"),
+                    rhs=w_exps[g][:, n0 : n0 + 2].rearrange("p n t i j -> p (n t i j)"),
                     start=True,
                     stop=True,
                 )
 
         def products_vector(g, t0, t1):
             prod = prods[g % NPROD]
+            nt = t1 - t0
             qs = slice(T * g + t0, T * g + t1)
-            wt = w_pss[g] if USE_WPS else w_exps[g]
-            for n in range(N_VEC):
-                di, dj = OFFSETS[n]
-                ia, ib = max(0, -di), 8 - max(0, di)
-                ja, jb = max(0, -dj), 7
-                for b in range(NB):
-                    nc.vector.tensor_tensor(
-                        out=prod[:, n, t0:t1, b, 0:56].rearrange("p t (i j) -> p t i j", j=7)[:, :, ia:ib, ja:jb],
-                        in0=x5[:, b, qs, ia + di : ib + di, ja + dj : jb + dj],
-                        in1=wt[:, n, t0:t1, 0:56].rearrange("p t (i j) -> p t i j", j=7)[:, :, ia:ib, ja:jb],
-                        op=ALU.mult,
-                    )
-                if dj <= 0:
-                    nc.vector.tensor_tensor(
-                        out=prod[:, n, t0:t1, :, 56 + ia : 56 + ib],
-                        in0=x5[:, :, qs, ia + di : ib + di, 7 + dj].rearrange("p b t i -> p t b i"),
-                        in1=wt[:, n, t0:t1, 56 + ia : 56 + ib].unsqueeze(2).to_broadcast([P, t1 - t0, NB, ib - ia]),
-                        op=ALU.mult,
-                    )
+            xg = x_sb[:, :, qs, :].rearrange("p b t s -> p t b s")
+            wt = w_pss[g]
+            for n, lo, hi, shift in ((0, 0, 64, 0), (1, 8, 64, -8), (2, 0, 56, 8)):
+                nc.vector.tensor_tensor(
+                    out=prod[:, n, t0:t1, :, lo:hi],
+                    in0=xg[:, :, :, lo + shift : hi + shift],
+                    in1=wt[:, n, t0:t1, lo:hi].unsqueeze(2).to_broadcast([P, nt, NB, hi - lo]),
+                    op=ALU.mult,
+                )
+            for b in range(NB):
+                nc.vector.tensor_tensor(
+                    out=prod[:, 3, t0:t1, b].rearrange("p t (i j) -> p t i j", j=8)[:, :, :, 1:8],
+                    in0=x5[:, b, qs, :, 0:7],
+                    in1=wt[:, 3, t0:t1].rearrange("p t (i j) -> p t i j", j=8)[:, :, :, 1:8],
+                    op=ALU.mult,
+                )
 
         def products_gpsimd(g, t0, t1):
             prod = prods[g % NPROD]
+            nt = t1 - t0
             qs = slice(T * g + t0, T * g + t1)
-            for n in range(N_VEC, NTAP):
-                di, dj = OFFSETS[n]
-                assert di == 0
-                ja, jb = max(0, -dj), 7
-                w4 = raw_w(g)[:, n, t0:t1]
-                for b in range(NB):
-                    nc.gpsimd.tensor_tensor(
-                        out=prod[:, n, t0:t1, b, 0:49].rearrange("p t (i j) -> p t i j", j=7)[:, :, :, ja:jb],
-                        in0=x5[:, b, qs, 0:7, ja + dj : jb + dj],
-                        in1=w4.rearrange("p t (i j) -> p t i j", j=7)[:, :, :, ja:jb],
-                        op=ALU.mult,
-                    )
+            p5 = prod[:, 4, t0:t1].rearrange("p t b (i j) -> p t b i j", j=8)
+            w4 = raw_w(g)[:, 4, t0:t1]
+            for b in range(NB):
                 nc.gpsimd.tensor_tensor(
-                    out=prod[:, n, t0:t1, :, 49 + ja : 49 + jb],
-                    in0=x5[:, :, qs, 7, ja + dj : jb + dj].rearrange("p b t j -> p t b j"),
-                    in1=w4[:, :, ja:jb].unsqueeze(2).to_broadcast([P, t1 - t0, NB, jb - ja]),
-                    op=ALU.mult,
+                    out=p5[:, :, b, 0:7, 0:7], in0=x5[:, b, qs, 0:7, 1:8], in1=w4, op=ALU.mult
                 )
-                if dj <= 0:
-                    nc.gpsimd.tensor_tensor(
-                        out=prod[:, n, t0:t1, :, 56:63],
-                        in0=x5[:, :, qs, 0:7, 7 + dj].rearrange("p b t i -> p t b i"),
-                        in1=w4[:, :, 0:49:7].unsqueeze(2).to_broadcast([P, t1 - t0, NB, 7]),
-                        op=ALU.mult,
-                    )
-                    nc.gpsimd.tensor_tensor(
-                        out=prod[:, n, t0:t1, :, 63:64],
-                        in0=x5[:, :, qs, 7:8, 7 + dj].rearrange("p b t i -> p t b i"),
-                        in1=w4[:, :, 0:1].unsqueeze(2).to_broadcast([P, t1 - t0, NB, 1]),
-                        op=ALU.mult,
-                    )
+            nc.gpsimd.tensor_tensor(
+                out=p5[:, :, :, 7, 0:7],
+                in0=x5[:, :, qs, 7, 1:8].rearrange("p b t j -> p t b j"),
+                in1=w4[:, :, 0, :].unsqueeze(2).to_broadcast([P, nt, NB, 7]),
+                op=ALU.mult,
+            )
 
         def add_taps(g, t0, t1):
             if t0 == 0:
@@ -218,16 +190,15 @@ def tile_lablock_w_kernel(tc, x, w, conv_w_words, conv_w_scales, conv_b, out):
 
         for g in range(E_AHEAD):
             expand(g)
-        if USE_WPS:
-            for g in range(W_AHEAD):
-                stage_w(g)
+        for g in range(W_AHEAD):
+            stage_w(g)
         for g in range(G):
             halves = ((0, T),) if g < G - 1 else ((0, 2), (2, T))
             for t0, t1 in halves:
                 products_gpsimd(g, t0, t1)
                 products_vector(g, t0, t1)
                 add_taps(g, t0, t1)
-            if USE_WPS and g + W_AHEAD < G:
+            if g + W_AHEAD < G:
                 stage_w(g + W_AHEAD)
             if g >= 1:
                 soft(g - 1)
@@ -261,26 +232,17 @@ def tile_lablock_w_kernel(tc, x, w, conv_w_words, conv_w_scales, conv_b, out):
                 )
 
         def quantise(g):
-            qs = slice(T * g, T * (g + 1))
-            u_t = u_ts[g]
-            grouped = work.tile([P, NB, 8, 8, T], BF16, name="grouped", align_bytes=64)
-            for b in range(NB):
-                nc.vector.tensor_tensor(
-                    out=grouped[:, b, :, 0:7, :],
-                    in0=u_t[:, :, b, 0:56].rearrange("p t (i j) -> p i j t", j=7),
-                    in1=x5[:, b, qs, :, 0:7].rearrange("p t i j -> p i j t"),
-                    op=ALU.mult,
-                )
-                nc.vector.tensor_tensor(
-                    out=grouped[:, b, :, 7, :],
-                    in0=u_t[:, :, b, 56:64].rearrange("p t i -> p i t"),
-                    in1=x5[:, b, qs, :, 7].rearrange("p t i -> p i t"),
-                    op=ALU.mult,
-                )
+            grouped = work.tile([P, NB, 64, T], BF16, name="grouped", align_bytes=64)
+            nc.vector.tensor_tensor(
+                out=grouped[:],
+                in0=u_ts[g][:].rearrange("p t b s -> p b s t"),
+                in1=x_sb[:, :, T * g : T * (g + 1), :].rearrange("p b t s -> p b s t"),
+                op=ALU.mult,
+            )
             nc.vector.quantize_mx(
                 out=x1_codes[:, g, :].bitcast(FP8X4),
                 scales=x1_planes[:, g, :],
-                in_=grouped[:].rearrange("p b i j t -> p (b i j t)"),
+                in_=grouped[:].rearrange("p b s t -> p (b s t)"),
             )
 
         def mx_pass(bank, k, g):

@@ -26,8 +26,11 @@ FLOPS = 2 * 128 * 4096 * 4096
 
 N_VEC = 4
 WAVE = 4
-E_AHEAD = 4
-W_AHEAD = 3
+W_SLOTS = ((0, 1), (2, 3))
+A_BANKS = (4, 5, 6)
+BIAS_BANK = 7
+ACC_BANKS = (0, 1, 2, 3)
+U_BANKS = (4, 5, 6, 7)
 LOADS = ((0, 2048, 2), (2048, 3072, 4), (3072, 3584, 8), (3584, 4096, 8))
 
 
@@ -36,7 +39,7 @@ def tile_lablock_w_kernel(tc, x, w, conv_w_words, conv_w_scales, conv_b, out):
     with ExitStack() as ctx:
         keep = ctx.enter_context(tc.tile_pool(name="keep", bufs=1))
         work = ctx.enter_context(tc.tile_pool(name="work", bufs=3))
-        psum = ctx.enter_context(tc.psum_pool(name="psum", bufs=4))
+        psum = ctx.enter_context(tc.psum_pool(name="psum", bufs=1))
         ctx.enter_context(tc.manual_schedule())
 
         w_words = keep.tile([P, G, O], U32, name="w_words", align_bytes=64)
@@ -96,53 +99,48 @@ def tile_lablock_w_kernel(tc, x, w, conv_w_words, conv_w_scales, conv_b, out):
                     in_=words_v[:, g0 : g0 + gstep, 4 * n0 : 4 * n1].bitcast(I32),
                 )
 
+        def psum_bank(i, shape, dtype, name):
+            return psum.tile(shape, dtype, name=name, tag="bank%d" % i)
+
         x5 = x_sb[:].rearrange("p b q (i j) -> p b q i j", j=8)
-        w_exps = {}
         w_pss = {}
         a_ts = {}
 
         def raw_w(g):
             return w_raw[:, g, :, 0:196].rearrange("p n (t i j) -> p n t i j", t=T, i=7)
 
-        def expand(g):
-            w_exp = work.tile([P, N_VEC, T, 8, 8], BF16, name="w_exp", bufs=E_AHEAD + 1)
-            w_exps[g] = w_exp
-            w4 = raw_w(g)[:, 0:N_VEC]
-            nc.scalar.copy(out=w_exp[:, :, :, 0:7, 0:7], in_=w4)
-            nc.scalar.copy(out=w_exp[:, :, :, 7, 0:7], in_=w4[:, :, :, 0, :])
-            nc.scalar.copy(out=w_exp[:, :, :, 0:7, 7], in_=w4[:, :, :, :, 0])
-            nc.scalar.copy(out=w_exp[:, :, :, 7, 7], in_=w4[:, :, :, 0, 0])
-
-        def stage_w(g):
-            w_ps = psum.tile([P, N_VEC, T, 64], BF16, name="w_ps", tag="acc")
-            w_pss[g] = w_ps
-            for n0 in range(0, N_VEC, 2):
-                nc.tensor.matmul(
-                    out=w_ps[:, n0 : n0 + 2].rearrange("p n t s -> p (n t s)"),
-                    lhsT=ident_b[:],
-                    rhs=w_exps[g][:, n0 : n0 + 2].rearrange("p n t i j -> p (n t i j)"),
-                    start=True,
-                    stop=True,
-                )
+        def spread(g):
+            w_pss[g] = []
+            for h in range(N_VEC // 2):
+                w_ps = psum_bank(W_SLOTS[g % 2][h], [P, 2, T, 8, 8], F32, "w_ps")
+                w_pss[g].append(w_ps)
+                src = raw_w(g)[:, 2 * h : 2 * h + 2]
+                for dst, part in (
+                    (w_ps[:, :, :, 0:7, 0:7], src),
+                    (w_ps[:, :, :, 7, 0:7], src[:, :, :, 0, :]),
+                    (w_ps[:, :, :, 0:7, 7], src[:, :, :, :, 0]),
+                    (w_ps[:, :, :, 7, 7], src[:, :, :, 0, 0]),
+                ):
+                    nc.tensor.matmul(out=dst, lhsT=ident_b[:], rhs=part, start=True, stop=True)
 
         def products_vector(g, t0, t1):
             prod = prods[g % NPROD]
             nt = t1 - t0
             qs = slice(T * g + t0, T * g + t1)
             xg = x_sb[:, :, qs, :].rearrange("p b t s -> p t b s")
-            wt = w_pss[g]
             for n, lo, hi, shift in ((0, 0, 64, 0), (1, 8, 64, -8), (2, 0, 56, 8)):
+                wt = w_pss[g][n // 2][:, n % 2, t0:t1].rearrange("p t i j -> p t (i j)")
                 nc.vector.tensor_tensor(
                     out=prod[:, n, t0:t1, :, lo:hi],
                     in0=xg[:, :, :, lo + shift : hi + shift],
-                    in1=wt[:, n, t0:t1, lo:hi].unsqueeze(2).to_broadcast([P, nt, NB, hi - lo]),
+                    in1=wt[:, :, lo:hi].unsqueeze(2).to_broadcast([P, nt, NB, hi - lo]),
                     op=ALU.mult,
                 )
             for b in range(NB):
                 nc.vector.tensor_tensor(
                     out=prod[:, 3, t0:t1, b].rearrange("p t (i j) -> p t i j", j=8)[:, :, :, 1:8],
                     in0=x5[:, b, qs, :, 0:7],
-                    in1=wt[:, 3, t0:t1].rearrange("p t (i j) -> p t i j", j=8)[:, :, :, 1:8],
+                    in1=w_pss[g][1][:, 1, t0:t1, :, 1:8],
                     op=ALU.mult,
                 )
 
@@ -165,7 +163,7 @@ def tile_lablock_w_kernel(tc, x, w, conv_w_words, conv_w_scales, conv_b, out):
 
         def add_taps(g, t0, t1):
             if t0 == 0:
-                a_ts[g] = psum.tile([P, 512], F32, name="a_t", tag="tp")
+                a_ts[g] = psum_bank(A_BANKS[g % 3], [P, 512], F32, "a_t")
             for t in range(t0, t1):
                 for n in range(NTAP):
                     nc.tensor.matmul(
@@ -188,33 +186,29 @@ def tile_lablock_w_kernel(tc, x, w, conv_w_words, conv_w_scales, conv_b, out):
                 accum_out=part_sum[:, g : g + 1],
             )
 
-        for g in range(E_AHEAD):
-            expand(g)
-        for g in range(W_AHEAD):
-            stage_w(g)
+        spread(0)
         for g in range(G):
+            if g + 1 < G:
+                spread(g + 1)
             halves = ((0, T),) if g < G - 1 else ((0, 2), (2, T))
             for t0, t1 in halves:
                 products_gpsimd(g, t0, t1)
                 products_vector(g, t0, t1)
                 add_taps(g, t0, t1)
-            if g + W_AHEAD < G:
-                stage_w(g + W_AHEAD)
             if g >= 1:
                 soft(g - 1)
             if g == 2:
-                bias_ps = psum.tile([P, P], BF16, name="bias_ps", tag="acc")
+                bias_ps = psum_bank(BIAS_BANK, [P, P], BF16, "bias_ps")
                 nc.tensor.transpose(bias_ps[:], bias_rows[:], ident_b[:])
             if g == 4:
                 nc.vector.tensor_copy(out=bias_sb[:], in_=bias_ps[:, 0:32])
-            if g + E_AHEAD < G:
-                expand(g + E_AHEAD)
         soft(G - 1)
 
         nc.vector.tensor_reduce(out=neg_max_all[:], in_=neg_max[:], axis=AX.X, op=ALU.min)
         nc.scalar.activation(out=factor[:], in_=neg_max[:], func=ACT.Exp, bias=neg_max_all[:], scale=-1.0)
-        nc.vector.tensor_tensor(out=weighted[:], in0=factor[:], in1=part_sum[:], op=ALU.mult)
-        nc.vector.tensor_reduce(out=total[:], in_=weighted[:], axis=AX.X, op=ALU.add)
+        nc.vector.scalar_tensor_tensor(
+            out=weighted[:], in0=factor[:], scalar=1.0, in1=part_sum[:], op0=ALU.mult, op1=ALU.mult, accum_out=total[:]
+        )
         nc.vector.reciprocal(out=recip[:], in_=total[:])
         nc.vector.tensor_scalar(out=coef[:], in0=factor[:], scalar1=recip[:], scalar2=None, op0=ALU.mult)
 
@@ -224,25 +218,30 @@ def tile_lablock_w_kernel(tc, x, w, conv_w_words, conv_w_scales, conv_b, out):
         def back(g):
             u = work.tile([P, 512], F32, name="u", tag="f32row", bufs=4)
             nc.scalar.activation(out=u[:], in_=e_sb[:, g, :], func=ACT.Copy, scale=coef[:, g : g + 1], bias=1.0)
-            u_t = psum.tile([P, T, NB, 64], F32, name="u_t", tag="tp")
+            u_t = psum_bank(U_BANKS[g % 4], [P, T, NB, 64], F32, "u_t")
             u_ts[g] = u_t
             for t in range(T):
                 nc.tensor.transpose(
                     u_t[:, t].rearrange("p b s -> p (b s)"), u[:, P * t : P * (t + 1)], ident_f[:]
                 )
 
-        def quantise(g):
+        groupeds = {}
+
+        def multiply(g):
             grouped = work.tile([P, NB, 64, T], BF16, name="grouped", align_bytes=64)
+            groupeds[g] = grouped
             nc.vector.tensor_tensor(
                 out=grouped[:],
                 in0=u_ts[g][:].rearrange("p t b s -> p b s t"),
                 in1=x_sb[:, :, T * g : T * (g + 1), :].rearrange("p b t s -> p b s t"),
                 op=ALU.mult,
             )
+
+        def quantise(g):
             nc.vector.quantize_mx(
                 out=x1_codes[:, g, :].bitcast(FP8X4),
                 scales=x1_planes[:, g, :],
-                in_=grouped[:].rearrange("p b s t -> p (b s t)"),
+                in_=groupeds[g][:].rearrange("p b s t -> p (b s t)"),
             )
 
         def mx_pass(bank, k, g):
@@ -262,10 +261,12 @@ def tile_lablock_w_kernel(tc, x, w, conv_w_words, conv_w_scales, conv_b, out):
                 mx_pass(bank, 0, g)
 
         for bank in range(WAVE):
-            accs[bank] = psum.tile([P, 4, P], F32, name="acc", tag="acc")
+            accs[bank] = psum_bank(ACC_BANKS[bank % 4], [P, 4, P], F32, "acc")
         for g in range(4):
             back(g)
         for pair in range(4):
+            multiply(2 * pair)
+            multiply(2 * pair + 1)
             quantise(2 * pair)
             quantise(2 * pair + 1)
             if 2 * pair + 4 < G:
@@ -277,12 +278,36 @@ def tile_lablock_w_kernel(tc, x, w, conv_w_words, conv_w_scales, conv_b, out):
         out_v = out.rearrange("b (k p) i j -> b p k (i j)", p=P)
         for bank in range(8):
             if bank >= WAVE:
-                accs[bank] = psum.tile([P, 4, P], F32, name="acc", tag="acc")
+                accs[bank] = psum_bank(ACC_BANKS[bank % 4], [P, 4, P], F32, "acc")
+            acc = accs[bank]
+            res = work.tile([P, 4, NB, 64], F32, name="res", tag="f32row", bufs=4)
+            if bank == 7:
+                for k in range(4):
+                    for g in range(G):
+                        mx_pass(bank, k, g)
+                    if k % 2 == 0:
+                        nc.vector.tensor_scalar(
+                            out=res[:, k].rearrange("p b s -> p (b s)"),
+                            in0=acc[:, k, :],
+                            scalar1=bias_sb[:, 4 * bank + k : 4 * bank + k + 1],
+                            scalar2=None,
+                            op0=ALU.add,
+                        )
+                    else:
+                        nc.scalar.activation(
+                            out=res[:, k].rearrange("p b s -> p (b s)"),
+                            in_=acc[:, k, :],
+                            func=ACT.Identity,
+                            bias=bias_sb[:, 4 * bank + k : 4 * bank + k + 1],
+                        )
+                        for b in range(NB):
+                            nc.sync.dma_start(
+                                out=out_v[b][:, 4 * bank + k - 1 : 4 * bank + k + 1, :], in_=res[:, k - 1 : k + 1, b, :]
+                            )
+                continue
             for k in range(1 if bank < WAVE else 0, 4):
                 for g in range(G):
                     mx_pass(bank, k, g)
-            acc = accs[bank]
-            res = work.tile([P, 4, NB, 64], F32, name="res", tag="f32row", bufs=4)
             if bank % 2 == 0:
                 nc.vector.tensor_tensor(
                     out=res[:].rearrange("p k b s -> p k (b s)"),

@@ -26,6 +26,7 @@ FLOPS = 2 * 128 * 4096 * 4096
 
 N_VEC = 4
 WAVE = 4
+N_RIGHT = 4
 W_SLOTS = ((0, 1), (2, 3))
 A_BANKS = (4, 5, 6)
 BIAS_BANK = 7
@@ -63,6 +64,7 @@ def tile_lablock_w_kernel(tc, x, w, conv_w_words, conv_w_scales, conv_b, out):
         recip = keep.tile([P, 1], F32, name="recip")
         coef = keep.tile([P, G], F32, name="coef")
         warm = keep.tile([P, 1], F32, name="warm")
+        w_right = [keep.tile([P, T, 8, 8], BF16, name="w_right%d" % k) for k in range(N_RIGHT)]
 
         nc.gpsimd.memset(bias_rows[:], 0.0)
         nc.scalar.dma_start(out=bias_rows[0:32, :], in_=conv_b.rearrange("(k p) -> k p", p=P))
@@ -74,7 +76,9 @@ def tile_lablock_w_kernel(tc, x, w, conv_w_words, conv_w_scales, conv_b, out):
             nc.vector.memset(prods[k][:, 1, :, :, 0:8], 0.0)
             nc.vector.memset(prods[k][:, 2, :, :, 56:64], 0.0)
             nc.vector.memset(prods[k][:, 3, :, :, 0:64:8], 0.0)
-            nc.gpsimd.memset(prods[k][:, 4, :, :, 7:64:8], 0.0)
+            nc.gpsimd.memset(prods[k][:, 4, :, :, 63:64], 0.0)
+        for k in range(N_RIGHT):
+            nc.gpsimd.memset(w_right[k][:], 0.0)
         for h in range(2):
             nc.vector.memset(planes[h][:].bitcast(I32), 0)
 
@@ -144,20 +148,19 @@ def tile_lablock_w_kernel(tc, x, w, conv_w_words, conv_w_scales, conv_b, out):
                     op=ALU.mult,
                 )
 
+        def expand_right(g):
+            nc.scalar.copy(out=w_right[g % N_RIGHT][:, :, 0:7, 0:7], in_=raw_w(g)[:, 4])
+            nc.scalar.copy(out=w_right[g % N_RIGHT][:, :, 7, 0:7], in_=raw_w(g)[:, 4, :, 0, :])
+
         def products_gpsimd(g, t0, t1):
-            prod = prods[g % NPROD]
             nt = t1 - t0
-            qs = slice(T * g + t0, T * g + t1)
-            p5 = prod[:, 4, t0:t1].rearrange("p t b (i j) -> p t b i j", j=8)
-            w4 = raw_w(g)[:, 4, t0:t1]
-            for b in range(NB):
-                nc.gpsimd.tensor_tensor(
-                    out=p5[:, :, b, 0:7, 0:7], in0=x5[:, b, qs, 0:7, 1:8], in1=w4, op=ALU.mult
-                )
             nc.gpsimd.tensor_tensor(
-                out=p5[:, :, :, 7, 0:7],
-                in0=x5[:, :, qs, 7, 1:8].rearrange("p b t j -> p t b j"),
-                in1=w4[:, :, 0, :].unsqueeze(2).to_broadcast([P, nt, NB, 7]),
+                out=prods[g % NPROD][:, 4, t0:t1, :, 0:63],
+                in0=x_sb[:, :, T * g + t0 : T * g + t1, 1:64].rearrange("p b t s -> p t b s"),
+                in1=w_right[g % N_RIGHT][:, t0:t1]
+                .rearrange("p t i j -> p t (i j)")[:, :, 0:63]
+                .unsqueeze(2)
+                .to_broadcast([P, nt, NB, 63]),
                 op=ALU.mult,
             )
 
@@ -186,6 +189,8 @@ def tile_lablock_w_kernel(tc, x, w, conv_w_words, conv_w_scales, conv_b, out):
                 accum_out=part_sum[:, g : g + 1],
             )
 
+        for g in range(N_RIGHT - 1):
+            expand_right(g)
         spread(0)
         for g in range(G):
             if g + 1 < G:
@@ -197,6 +202,8 @@ def tile_lablock_w_kernel(tc, x, w, conv_w_words, conv_w_scales, conv_b, out):
                 add_taps(g, t0, t1)
             if g >= 1:
                 soft(g - 1)
+            if g + N_RIGHT - 1 < G:
+                expand_right(g + N_RIGHT - 1)
             if g == 2:
                 bias_ps = psum_bank(BIAS_BANK, [P, P], BF16, "bias_ps")
                 nc.tensor.transpose(bias_ps[:], bias_rows[:], ident_b[:])

@@ -26,13 +26,14 @@ FLOPS = 2 * 128 * 4096 * 4096
 
 N_VEC = 4
 WAVE = 4
+PIECE_COLS = (0, 512, 1024, 1536, 2048, 2560, 3072, 3584, 3968, 4096)
 N_RIGHT = 4
 W_SLOTS = ((0, 1), (2, 3))
 A_BANKS = (4, 5, 6)
 BIAS_BANK = 7
 ACC_BANKS = (0, 1, 2, 3)
 U_BANKS = (4, 5, 6, 7)
-LOADS = ((0, 2048, 2), (2048, 3072, 4), (3072, 3584, 8), (3584, 4096, 8))
+LOADS = ((0, 2048, 2), (2048, 3072, 4), (3072, 4096, 4))
 
 
 def tile_lablock_w_kernel(tc, x, w, conv_w_words, conv_w_scales, conv_b, out):
@@ -55,27 +56,29 @@ def tile_lablock_w_kernel(tc, x, w, conv_w_words, conv_w_scales, conv_b, out):
         ident_b = keep.tile([P, P], BF16, name="ident_b")
         bias_rows = keep.tile([P, P], BF16, name="bias_rows")
         bias_sb = keep.tile([P, 32], F32, name="bias_sb")
-        neg_max = keep.tile([P, G], F32, name="neg_max")
-        part_sum = keep.tile([P, G], F32, name="part_sum")
+        neg_max = keep.tile([P, G + 1], F32, name="neg_max")
+        part_sum = keep.tile([P, G + 1], F32, name="part_sum")
         neg_max_all = keep.tile([P, 1], F32, name="neg_max_all")
-        factor = keep.tile([P, G], F32, name="factor")
-        weighted = keep.tile([P, G], F32, name="weighted")
+        factor = keep.tile([P, G + 1], F32, name="factor")
+        weighted = keep.tile([P, G + 1], F32, name="weighted")
         total = keep.tile([P, 1], F32, name="total")
         recip = keep.tile([P, 1], F32, name="recip")
-        coef = keep.tile([P, G], F32, name="coef")
+        coef = keep.tile([P, G + 1], F32, name="coef")
         warm = keep.tile([P, 1], F32, name="warm")
+        zero_b = keep.tile([P, T * 8], BF16, name="zero_b")
         w_right = [keep.tile([P, T, 8, 8], BF16, name="w_right%d" % k) for k in range(N_RIGHT)]
 
         nc.gpsimd.memset(bias_rows[:], 0.0)
         nc.scalar.dma_start(out=bias_rows[0:32, :], in_=conv_b.rearrange("(k p) -> k p", p=P))
         nc.vector.memset(warm[:], 0.0)
+        nc.vector.memset(zero_b[:], 0.0)
         nc.scalar.activation(out=warm[:], in_=warm[:], func=ACT.Exp)
         make_identity(nc, ident_b[:])
         make_identity(nc, ident_f[:])
         for k in range(NPROD):
             nc.vector.memset(prods[k][:, 1, :, :, 0:8], 0.0)
             nc.vector.memset(prods[k][:, 2, :, :, 56:64], 0.0)
-            nc.vector.memset(prods[k][:, 3, :, :, 0:64:8], 0.0)
+            nc.vector.memset(prods[k][:, 3, :, :, 0:1], 0.0)
             nc.gpsimd.memset(prods[k][:, 4, :, :, 63:64], 0.0)
         for k in range(N_RIGHT):
             nc.gpsimd.memset(w_right[k][:], 0.0)
@@ -106,7 +109,7 @@ def tile_lablock_w_kernel(tc, x, w, conv_w_words, conv_w_scales, conv_b, out):
         def psum_bank(i, shape, dtype, name):
             return psum.tile(shape, dtype, name=name, tag="bank%d" % i)
 
-        x5 = x_sb[:].rearrange("p b q (i j) -> p b q i j", j=8)
+        e_flat = e_sb[:].rearrange("p g c -> p (g c)")
         w_pss = {}
         a_ts = {}
 
@@ -126,25 +129,25 @@ def tile_lablock_w_kernel(tc, x, w, conv_w_words, conv_w_scales, conv_b, out):
                     (w_ps[:, :, :, 7, 7], src[:, :, :, 0, 0]),
                 ):
                     nc.tensor.matmul(out=dst, lhsT=ident_b[:], rhs=part, start=True, stop=True)
+            nc.tensor.matmul(
+                out=w_pss[g][1][:, 1, :, :, 0],
+                lhsT=ident_b[:],
+                rhs=zero_b[:].rearrange("p (t i) -> p t i", t=T),
+                start=True,
+                stop=True,
+            )
 
         def products_vector(g, t0, t1):
             prod = prods[g % NPROD]
             nt = t1 - t0
             qs = slice(T * g + t0, T * g + t1)
             xg = x_sb[:, :, qs, :].rearrange("p b t s -> p t b s")
-            for n, lo, hi, shift in ((0, 0, 64, 0), (1, 8, 64, -8), (2, 0, 56, 8)):
+            for n, lo, hi, shift in ((0, 0, 64, 0), (1, 8, 64, -8), (2, 0, 56, 8), (3, 1, 64, -1)):
                 wt = w_pss[g][n // 2][:, n % 2, t0:t1].rearrange("p t i j -> p t (i j)")
                 nc.vector.tensor_tensor(
                     out=prod[:, n, t0:t1, :, lo:hi],
                     in0=xg[:, :, :, lo + shift : hi + shift],
                     in1=wt[:, :, lo:hi].unsqueeze(2).to_broadcast([P, nt, NB, hi - lo]),
-                    op=ALU.mult,
-                )
-            for b in range(NB):
-                nc.vector.tensor_tensor(
-                    out=prod[:, 3, t0:t1, b].rearrange("p t (i j) -> p t i j", j=8)[:, :, :, 1:8],
-                    in0=x5[:, b, qs, :, 0:7],
-                    in1=w_pss[g][1][:, 1, t0:t1, :, 1:8],
                     op=ALU.mult,
                 )
 
@@ -165,12 +168,12 @@ def tile_lablock_w_kernel(tc, x, w, conv_w_words, conv_w_scales, conv_b, out):
             )
 
         def add_taps(g, t0, t1):
-            if t0 == 0:
-                a_ts[g] = psum_bank(A_BANKS[g % 3], [P, 512], F32, "a_t")
+            piece = g if t0 == 0 else g + 1
+            a_ts[piece] = psum_bank(A_BANKS[piece % 3], [P, P * (t1 - t0)], F32, "a_t")
             for t in range(t0, t1):
                 for n in range(NTAP):
                     nc.tensor.matmul(
-                        out=a_ts[g][:, P * t : P * (t + 1)],
+                        out=a_ts[piece][:, P * (t - t0) : P * (t - t0 + 1)],
                         lhsT=prods[g % NPROD][:, n, t].rearrange("p b s -> p (b s)"),
                         rhs=ident_f[:],
                         is_transpose=True,
@@ -181,7 +184,7 @@ def tile_lablock_w_kernel(tc, x, w, conv_w_words, conv_w_scales, conv_b, out):
         def soft(g):
             nc.vector.tensor_reduce(out=neg_max[:, g : g + 1], in_=a_ts[g][:], axis=AX.X, op=ALU.max, negate=True)
             nc.scalar.activation(
-                out=e_sb[:, g, :],
+                out=e_flat[:, PIECE_COLS[g] : PIECE_COLS[g + 1]],
                 in_=a_ts[g][:],
                 func=ACT.Exp,
                 bias=neg_max[:, g : g + 1],
@@ -195,7 +198,7 @@ def tile_lablock_w_kernel(tc, x, w, conv_w_words, conv_w_scales, conv_b, out):
         for g in range(G):
             if g + 1 < G:
                 spread(g + 1)
-            halves = ((0, T),) if g < G - 1 else ((0, 2), (2, T))
+            halves = ((0, T),) if g < G - 1 else ((0, 3), (3, T))
             for t0, t1 in halves:
                 products_gpsimd(g, t0, t1)
                 products_vector(g, t0, t1)
@@ -210,6 +213,7 @@ def tile_lablock_w_kernel(tc, x, w, conv_w_words, conv_w_scales, conv_b, out):
             if g == 4:
                 nc.vector.tensor_copy(out=bias_sb[:], in_=bias_ps[:, 0:32])
         soft(G - 1)
+        soft(G)
 
         nc.vector.tensor_reduce(out=neg_max_all[:], in_=neg_max[:], axis=AX.X, op=ALU.min)
         nc.scalar.activation(out=factor[:], in_=neg_max[:], func=ACT.Exp, bias=neg_max_all[:], scale=-1.0)
@@ -223,8 +227,16 @@ def tile_lablock_w_kernel(tc, x, w, conv_w_words, conv_w_scales, conv_b, out):
         accs = {}
 
         def back(g):
-            u = work.tile([P, 512], F32, name="u", tag="f32row", bufs=4)
-            nc.scalar.activation(out=u[:], in_=e_sb[:, g, :], func=ACT.Copy, scale=coef[:, g : g + 1], bias=1.0)
+            u = work.tile([P, 512], F32, name="u", bufs=4)
+            for piece in (g,) if g < G - 1 else (g, g + 1):
+                c0, c1 = PIECE_COLS[piece], PIECE_COLS[piece + 1]
+                nc.scalar.activation(
+                    out=u[:, c0 - 512 * g : c1 - 512 * g],
+                    in_=e_flat[:, c0:c1],
+                    func=ACT.Copy,
+                    scale=coef[:, piece : piece + 1],
+                    bias=1.0,
+                )
             u_t = psum_bank(U_BANKS[g % 4], [P, T, NB, 64], F32, "u_t")
             u_ts[g] = u_t
             for t in range(T):
@@ -283,11 +295,12 @@ def tile_lablock_w_kernel(tc, x, w, conv_w_words, conv_w_scales, conv_b, out):
             wave(2 * pair + 1)
 
         out_v = out.rearrange("b (k p) i j -> b p k (i j)", p=P)
+        store_queues = (nc.sync, nc.scalar)
         for bank in range(8):
             if bank >= WAVE:
                 accs[bank] = psum_bank(ACC_BANKS[bank % 4], [P, 4, P], F32, "acc")
             acc = accs[bank]
-            res = work.tile([P, 4, NB, 64], F32, name="res", tag="f32row", bufs=4)
+            res = work.tile([P, 4, NB, 64], F32, name="res", bufs=6)
             if bank == 7:
                 for k in range(4):
                     for g in range(G):
@@ -308,7 +321,7 @@ def tile_lablock_w_kernel(tc, x, w, conv_w_words, conv_w_scales, conv_b, out):
                             bias=bias_sb[:, 4 * bank + k : 4 * bank + k + 1],
                         )
                         for b in range(NB):
-                            nc.sync.dma_start(
+                            store_queues[b].dma_start(
                                 out=out_v[b][:, 4 * bank + k - 1 : 4 * bank + k + 1, :], in_=res[:, k - 1 : k + 1, b, :]
                             )
                 continue
@@ -331,4 +344,4 @@ def tile_lablock_w_kernel(tc, x, w, conv_w_words, conv_w_scales, conv_b, out):
                         bias=bias_sb[:, 4 * bank + k : 4 * bank + k + 1],
                     )
             for b in range(NB):
-                nc.sync.dma_start(out=out_v[b][:, 4 * bank : 4 * bank + 4, :], in_=res[:, :, b, :])
+                store_queues[b].dma_start(out=out_v[b][:, 4 * bank : 4 * bank + 4, :], in_=res[:, :, b, :])

@@ -33,7 +33,7 @@ A_BANKS = (4, 5, 6)
 BIAS_BANK = 7
 ACC_BANKS = (0, 1, 2, 3)
 U_BANKS = (4, 5, 6, 7)
-LOADS = ((0, 2048, 2), (2048, 3072, 4), (3072, 4096, 4))
+LOADS = ((0, 2048, 2), (2048, 3072, 4), (3072, 3584, 8), (3584, 4096, 8))
 
 
 def tile_lablock_w_kernel(tc, x, w, conv_w_words, conv_w_scales, conv_b, out):
@@ -92,12 +92,6 @@ def tile_lablock_w_kernel(tc, x, w, conv_w_words, conv_w_scales, conv_b, out):
             nc.sync.dma_start(
                 out=x_sb[:, :, T * g : T * (g + 1), :].rearrange("p b t s -> p b (t s)"), in_=x_v[g]
             )
-        for h in range(2):
-            for q in range(4):
-                nc.sync.dma_start(
-                    out=planes[h][32 * q : 32 * q + 16, :].bitcast(I32),
-                    in_=conv_w_scales[4 * h : 4 * h + 4, 4 * q : 4 * q + 4, :].bitcast(I32),
-                )
         words_v = conv_w_words.rearrange("g p n t -> p g (n t)")
         for n0, n1, gstep in LOADS:
             for g0 in range(0, G, gstep):
@@ -167,6 +161,13 @@ def tile_lablock_w_kernel(tc, x, w, conv_w_words, conv_w_scales, conv_b, out):
                 op=ALU.mult,
             )
 
+        def load_scales(k):
+            h, q = divmod(k, 4)
+            nc.gpsimd.dma_start(
+                out=planes[h][32 * q : 32 * q + 16, :].bitcast(F32),
+                in_=conv_w_scales[4 * h : 4 * h + 4, 4 * q : 4 * q + 4, :].bitcast(F32),
+            )
+
         def add_taps(g, t0, t1):
             piece = g if t0 == 0 else g + 1
             a_ts[piece] = psum_bank(A_BANKS[piece % 3], [P, P * (t1 - t0)], F32, "a_t")
@@ -203,6 +204,7 @@ def tile_lablock_w_kernel(tc, x, w, conv_w_words, conv_w_scales, conv_b, out):
                 products_gpsimd(g, t0, t1)
                 products_vector(g, t0, t1)
                 add_taps(g, t0, t1)
+            load_scales(g)
             if g >= 1:
                 soft(g - 1)
             if g + N_RIGHT - 1 < G:
@@ -295,7 +297,7 @@ def tile_lablock_w_kernel(tc, x, w, conv_w_words, conv_w_scales, conv_b, out):
             wave(2 * pair + 1)
 
         out_v = out.rearrange("b (k p) i j -> b p k (i j)", p=P)
-        store_queues = (nc.sync, nc.scalar)
+        store_queues = (nc.sync, nc.sync)
         for bank in range(8):
             if bank >= WAVE:
                 accs[bank] = psum_bank(ACC_BANKS[bank % 4], [P, 4, P], F32, "acc")

@@ -33,7 +33,7 @@ A_BANKS = (4, 5, 6)
 BIAS_BANK = 7
 ACC_BANKS = (0, 1, 2, 3)
 U_BANKS = (4, 5, 6, 7)
-LOADS = ((0, 2048, 2), (2048, 3072, 4), (3072, 3584, 8), (3584, 4096, 8))
+HALF = 4
 
 
 def tile_lablock_w_kernel(tc, x, w, conv_w_words, conv_w_scales, conv_b, out):
@@ -93,12 +93,13 @@ def tile_lablock_w_kernel(tc, x, w, conv_w_words, conv_w_scales, conv_b, out):
                 out=x_sb[:, :, T * g : T * (g + 1), :].rearrange("p b t s -> p b (t s)"), in_=x_v[g]
             )
         words_v = conv_w_words.rearrange("g p n t -> p g (n t)")
-        for n0, n1, gstep in LOADS:
-            for g0 in range(0, G, gstep):
-                nc.sync.dma_start(
-                    out=w_words[:, g0 : g0 + gstep, n0:n1].bitcast(I32),
-                    in_=words_v[:, g0 : g0 + gstep, 4 * n0 : 4 * n1].bitcast(I32),
-                )
+        for g in range(HALF):
+            nc.sync.dma_start(out=w_words[:, g, :].bitcast(I32), in_=words_v[:, g, :].bitcast(I32))
+        for n0 in range(0, O, 1024):
+            nc.sync.dma_start(
+                out=w_words[:, HALF:G, n0 : n0 + 1024].bitcast(I32),
+                in_=words_v[:, HALF:G, 4 * n0 : 4 * (n0 + 1024)].bitcast(I32),
+            )
 
         def psum_bank(i, shape, dtype, name):
             return psum.tile(shape, dtype, name=name, tag="bank%d" % i)
@@ -265,85 +266,85 @@ def tile_lablock_w_kernel(tc, x, w, conv_w_words, conv_w_scales, conv_b, out):
                 in_=groupeds[g][:].rearrange("p b s t -> p (b s t)"),
             )
 
-        def mx_pass(bank, k, g):
-            cols = slice(P * (4 * bank + k), P * (4 * bank + k + 1))
+        half_flat = [prods[k][:].rearrange("p n t b s -> p (n t b s)") for k in range(2)]
+
+        def half_sum(unit):
+            return half_flat[unit // 5][:, 512 * (unit % 5) : 512 * (unit % 5 + 1)].rearrange("p (k c) -> p k c", k=4)
+
+        def mx_pass(acc, unit, k, g):
+            cols = slice(P * (4 * unit + k), P * (4 * unit + k + 1))
             nc.tensor.matmul_mx(
-                out=accs[bank][:, k, :],
+                out=acc[:, k, :],
                 lhsT=w_words[:, g, cols].bitcast(FP8X4),
                 lhsT_scale=planes[g // 4][4 * (g % 4) : P, cols],
                 rhs=x1_codes[:, g, :].bitcast(FP8X4),
                 rhs_scale=x1_planes[:, g, :],
-                start=(g == 0),
-                stop=(g == G - 1),
+                start=(g % HALF == 0),
+                stop=(g % HALF == HALF - 1),
             )
 
         def wave(g):
-            for bank in range(WAVE):
-                mx_pass(bank, 0, g)
+            for unit in range(WAVE):
+                mx_pass(accs[unit], unit, 0, g)
 
-        for bank in range(WAVE):
-            accs[bank] = psum_bank(ACC_BANKS[bank % 4], [P, 4, P], F32, "acc")
+        for unit in range(WAVE):
+            accs[unit] = psum_bank(ACC_BANKS[unit], [P, 4, P], F32, "acc")
         for g in range(4):
             back(g)
-        for pair in range(4):
+        for pair in range(2):
             multiply(2 * pair)
             multiply(2 * pair + 1)
             quantise(2 * pair)
             quantise(2 * pair + 1)
-            if 2 * pair + 4 < G:
-                back(2 * pair + 4)
-                back(2 * pair + 5)
+            back(2 * pair + 4)
+            back(2 * pair + 5)
             wave(2 * pair)
             wave(2 * pair + 1)
+        for pair in range(2, 4):
+            multiply(2 * pair)
+            multiply(2 * pair + 1)
+            quantise(2 * pair)
+            quantise(2 * pair + 1)
+
+        for unit in range(8):
+            if unit >= WAVE:
+                accs[unit] = psum_bank(ACC_BANKS[unit % 4], [P, 4, P], F32, "acc")
+            for k in range(1 if unit < WAVE else 0, 4):
+                for g in range(HALF):
+                    mx_pass(accs[unit], unit, k, g)
+            for k in range(4):
+                nc.scalar.activation(
+                    out=half_sum(unit)[:, k, :],
+                    in_=accs[unit][:, k, :],
+                    func=ACT.Identity,
+                    bias=bias_sb[:, 4 * unit + k : 4 * unit + k + 1],
+                )
 
         out_v = out.rearrange("b (k p) i j -> b p k (i j)", p=P)
-        store_queues = (nc.sync, nc.sync)
-        for bank in range(8):
-            if bank >= WAVE:
-                accs[bank] = psum_bank(ACC_BANKS[bank % 4], [P, 4, P], F32, "acc")
-            acc = accs[bank]
+        for unit in range(8):
+            acc = psum_bank((unit + 4) % 8, [P, 4, P], F32, "acc")
             res = work.tile([P, 4, NB, 64], F32, name="res", bufs=6)
-            if bank == 7:
+            if unit < 7:
                 for k in range(4):
-                    for g in range(G):
-                        mx_pass(bank, k, g)
-                    if k % 2 == 0:
-                        nc.vector.tensor_scalar(
-                            out=res[:, k].rearrange("p b s -> p (b s)"),
-                            in0=acc[:, k, :],
-                            scalar1=bias_sb[:, 4 * bank + k : 4 * bank + k + 1],
-                            scalar2=None,
-                            op0=ALU.add,
-                        )
-                    else:
-                        nc.scalar.activation(
-                            out=res[:, k].rearrange("p b s -> p (b s)"),
-                            in_=acc[:, k, :],
-                            func=ACT.Identity,
-                            bias=bias_sb[:, 4 * bank + k : 4 * bank + k + 1],
-                        )
-                        for b in range(NB):
-                            store_queues[b].dma_start(
-                                out=out_v[b][:, 4 * bank + k - 1 : 4 * bank + k + 1, :], in_=res[:, k - 1 : k + 1, b, :]
-                            )
-                continue
-            for k in range(1 if bank < WAVE else 0, 4):
-                for g in range(G):
-                    mx_pass(bank, k, g)
-            if bank % 2 == 0:
+                    for g in range(HALF, G):
+                        mx_pass(acc, unit, k, g)
                 nc.vector.tensor_tensor(
-                    out=res[:].rearrange("p k b s -> p k (b s)"),
-                    in0=acc[:],
-                    in1=bias_sb[:, 4 * bank : 4 * bank + 4].unsqueeze(2).to_broadcast([P, 4, P]),
-                    op=ALU.add,
+                    out=res[:].rearrange("p k b s -> p k (b s)"), in0=acc[:], in1=half_sum(unit), op=ALU.add
                 )
+                for b in range(NB):
+                    nc.sync.dma_start(out=out_v[b][:, 4 * unit : 4 * unit + 4, :], in_=res[:, :, b, :])
             else:
                 for k in range(4):
-                    nc.scalar.activation(
+                    for g in range(HALF, G):
+                        mx_pass(acc, unit, k, g)
+                    nc.vector.tensor_tensor(
                         out=res[:, k].rearrange("p b s -> p (b s)"),
-                        in_=acc[:, k, :],
-                        func=ACT.Identity,
-                        bias=bias_sb[:, 4 * bank + k : 4 * bank + k + 1],
+                        in0=acc[:, k, :],
+                        in1=half_sum(unit)[:, k, :],
+                        op=ALU.add,
                     )
-            for b in range(NB):
-                store_queues[b].dma_start(out=out_v[b][:, 4 * bank : 4 * bank + 4, :], in_=res[:, :, b, :])
+                    if k % 2 == 1:
+                        for b in range(NB):
+                            nc.sync.dma_start(
+                                out=out_v[b][:, 4 * unit + k - 1 : 4 * unit + k + 1, :], in_=res[:, k - 1 : k + 1, b, :]
+                            )

@@ -88,10 +88,13 @@ def tile_lablock_w_kernel(tc, x, w, conv_w_words, conv_w_scales, conv_b, out):
         x_v = x.rearrange("b (g p t) i j -> g p b (t i j)", g=G, p=P, t=T)
         w_v = w.rearrange("n (g p t) r s -> g p n (t r s)", g=G, p=P, t=T)
         for g in range(G):
-            nc.sync.dma_start(out=w_raw[:, g, :, 0:196], in_=w_v[g])
+            first = 2 if g == 0 else NTAP
+            nc.sync.dma_start(out=w_raw[:, g, 0:first, 0:196], in_=w_v[g][:, 0:first])
             nc.sync.dma_start(
                 out=x_sb[:, :, T * g : T * (g + 1), :].rearrange("p b t s -> p b (t s)"), in_=x_v[g]
             )
+            if first < NTAP:
+                nc.sync.dma_start(out=w_raw[:, g, first:NTAP, 0:196], in_=w_v[g][:, first:NTAP])
         words_v = conv_w_words.rearrange("g p n t -> p g (n t)")
         for g in range(HALF):
             nc.sync.dma_start(out=w_words[:, g, :].bitcast(I32), in_=words_v[:, g, :].bitcast(I32))

from contextlib import ExitStack

from concourse import mybir
from concourse.masks import make_identity

F32 = mybir.dt.float32
BF16 = mybir.dt.bfloat16
I32 = mybir.dt.int32
U32 = mybir.dt.uint32
U8 = mybir.dt.uint8
FP8X4 = mybir.dt.float8_e4m3fn_x4
ALU = mybir.AluOpType
ACT = mybir.ActivationFunctionType
AX = mybir.AxisListType

P = 128
G = 8
T = 4
NB = 2
NTAP = 5
O = 4096
W_PITCH = 208
NPROD = 3

FLOPS = 2 * 128 * 4096 * 4096

N_VEC = 4
WAVE = 4
PIECE_COLS = (0, 512, 1024, 1536, 2048, 2560, 3072, 3584, 3968, 4096)
N_RIGHT = 4
W_SLOTS = ((0, 1), (2, 3))
A_BANKS = (4, 5, 6)
BIAS_BANK = 7
ACC_BANKS = (0, 1, 2, 3)
U_BANKS = (4, 5, 6, 7)
HALF = 4


def tile_lablock_w_kernel(tc, x, w, conv_w_words, conv_w_scales, conv_b, out):
    nc = tc.nc
    with ExitStack() as ctx:
        keep = ctx.enter_context(tc.tile_pool(name="keep", bufs=1))
        work = ctx.enter_context(tc.tile_pool(name="work", bufs=3))
        psum = ctx.enter_context(tc.psum_pool(name="psum", bufs=1))
        ctx.enter_context(tc.manual_schedule())

        w_words = keep.tile([P, G, O], U32, name="w_words", align_bytes=64)
        planes = [keep.tile([P, O], U8, name="planes%d" % h, align_bytes=64) for h in range(2)]
        x_sb = keep.tile([P, NB, G * T, 64], BF16, name="x_sb")
        w_raw = keep.tile([P, G, NTAP, W_PITCH], BF16, name="w_raw")
        prods = [keep.tile([P, NTAP, T, NB, 64], F32, name="prod%d" % k) for k in range(NPROD)]
        e_sb = keep.tile([P, G, 512], F32, name="e_sb")
        x1_codes = keep.tile([P, G, P], U32, name="x1_codes", align_bytes=64)
        x1_planes = keep.tile([P, G, P], U8, name="x1_planes", align_bytes=64)
        ident_f = keep.tile([P, P], F32, name="ident_f")
        ident_b = keep.tile([P, P], BF16, name="ident_b")
        bias_rows = keep.tile([P, P], BF16, name="bias_rows")
        bias_sb = keep.tile([P, 32], F32, name="bias_sb")
        neg_max = keep.tile([P, G + 1], F32, name="neg_max")
        part_sum = keep.tile([P, G + 1], F32, name="part_sum")
        neg_max_all = keep.tile([P, 1], F32, name="neg_max_all")
        factor = keep.tile([P, G + 1], F32, name="factor")
        weighted = keep.tile([P, G + 1], F32, name="weighted")
        total = keep.tile([P, 1], F32, name="total")
        recip = keep.tile([P, 1], F32, name="recip")
        coef = keep.tile([P, G + 1], F32, name="coef")
        warm = keep.tile([P, 1], F32, name="warm")
        zero_b = keep.tile([P, T * 8], BF16, name="zero_b")
        w_right = [keep.tile([P, T, 8, 8], BF16, name="w_right%d" % k) for k in range(N_RIGHT)]

        nc.gpsimd.memset(bias_rows[:], 0.0)
        nc.scalar.dma_start(out=bias_rows[0:32, :], in_=conv_b.rearrange("(k p) -> k p", p=P))
        nc.vector.memset(warm[:], 0.0)
        nc.vector.memset(zero_b[:], 0.0)
        nc.scalar.activation(out=warm[:], in_=warm[:], func=ACT.Exp)
        make_identity(nc, ident_b[:])
        make_identity(nc, ident_f[:])
        for k in range(NPROD):
            nc.vector.memset(prods[k][:, 1, :, :, 0:8], 0.0)
            nc.vector.memset(prods[k][:, 2, :, :, 56:64], 0.0)
            nc.vector.memset(prods[k][:, 3, :, :, 0:1], 0.0)
            nc.gpsimd.memset(prods[k][:, 4, :, :, 63:64], 0.0)
        for k in range(N_RIGHT):
            nc.gpsimd.memset(w_right[k][:], 0.0)
        for h in range(2):
            nc.vector.memset(planes[h][:].bitcast(I32), 0)

        x_v = x.rearrange("b (g p t) i j -> g p b (t i j)", g=G, p=P, t=T)
        w_v = w.rearrange("n (g p t) r s -> g p n (t r s)", g=G, p=P, t=T)
        for g in range(G):
            first = 2 if g == 0 else NTAP
            nc.sync.dma_start(out=w_raw[:, g, 0:first, 0:196], in_=w_v[g][:, 0:first])
            nc.sync.dma_start(
                out=x_sb[:, :, T * g : T * (g + 1), :].rearrange("p b t s -> p b (t s)"), in_=x_v[g]
            )
            if first < NTAP:
                nc.sync.dma_start(out=w_raw[:, g, first:NTAP, 0:196], in_=w_v[g][:, first:NTAP])
        words_v = conv_w_words.rearrange("g p n t -> p g (n t)")
        for g in range(HALF):
            nc.sync.dma_start(out=w_words[:, g, :].bitcast(I32), in_=words_v[:, g, :].bitcast(I32))
        for n0 in range(0, O, 1024):
            nc.sync.dma_start(
                out=w_words[:, HALF:G, n0 : n0 + 1024].bitcast(I32),
                in_=words_v[:, HALF:G, 4 * n0 : 4 * (n0 + 1024)].bitcast(I32),
            )

        def psum_bank(i, shape, dtype, name):
            return psum.tile(shape, dtype, name=name, tag="bank%d" % i)

        e_flat = e_sb[:].rearrange("p g c -> p (g c)")
        w_pss = {}
        a_ts = {}

        def raw_w(g):
            return w_raw[:, g, :, 0:196].rearrange("p n (t i j) -> p n t i j", t=T, i=7)

        def spread(g):
            w_pss[g] = []
            for h in range(N_VEC // 2):
                w_ps = psum_bank(W_SLOTS[g % 2][h], [P, 2, T, 8, 8], F32, "w_ps")
                w_pss[g].append(w_ps)
                src = raw_w(g)[:, 2 * h : 2 * h + 2]
                for dst, part in (
                    (w_ps[:, :, :, 0:7, 0:7], src),
                    (w_ps[:, :, :, 7, 0:7], src[:, :, :, 0, :]),
                    (w_ps[:, :, :, 0:7, 7], src[:, :, :, :, 0]),
                    (w_ps[:, :, :, 7, 7], src[:, :, :, 0, 0]),
                ):
                    nc.tensor.matmul(out=dst, lhsT=ident_b[:], rhs=part, start=True, stop=True)
            nc.tensor.matmul(
                out=w_pss[g][1][:, 1, :, :, 0],
                lhsT=ident_b[:],
                rhs=zero_b[:].rearrange("p (t i) -> p t i", t=T),
                start=True,
                stop=True,
            )

        def products_vector(g, t0, t1):
            prod = prods[g % NPROD]
            nt = t1 - t0
            qs = slice(T * g + t0, T * g + t1)
            xg = x_sb[:, :, qs, :].rearrange("p b t s -> p t b s")
            for n, lo, hi, shift in ((0, 0, 64, 0), (1, 8, 64, -8), (2, 0, 56, 8), (3, 1, 64, -1)):
                wt = w_pss[g][n // 2][:, n % 2, t0:t1].rearrange("p t i j -> p t (i j)")
                nc.vector.tensor_tensor(
                    out=prod[:, n, t0:t1, :, lo:hi],
                    in0=xg[:, :, :, lo + shift : hi + shift],
                    in1=wt[:, :, lo:hi].unsqueeze(2).to_broadcast([P, nt, NB, hi - lo]),
                    op=ALU.mult,
                )

        def expand_right(g):
            nc.scalar.copy(out=w_right[g % N_RIGHT][:, :, 0:7, 0:7], in_=raw_w(g)[:, 4])
            nc.scalar.copy(out=w_right[g % N_RIGHT][:, :, 7, 0:7], in_=raw_w(g)[:, 4, :, 0, :])

        def products_gpsimd(g, t0, t1):
            nt = t1 - t0
            nc.gpsimd.tensor_tensor(
                out=prods[g % NPROD][:, 4, t0:t1, :, 0:63],
                in0=x_sb[:, :, T * g + t0 : T * g + t1, 1:64].rearrange("p b t s -> p t b s"),
                in1=w_right[g % N_RIGHT][:, t0:t1]
                .rearrange("p t i j -> p t (i j)")[:, :, 0:63]
                .unsqueeze(2)
                .to_broadcast([P, nt, NB, 63]),
                op=ALU.mult,
            )

        def load_scales(k):
            h, q = divmod(k, 4)
            nc.gpsimd.dma_start(
                out=planes[h][32 * q : 32 * q + 16, :].bitcast(F32),
                in_=conv_w_scales[4 * h : 4 * h + 4, 4 * q : 4 * q + 4, :].bitcast(F32),
            )

        def add_taps(g, t0, t1):
            piece = g if t0 == 0 else g + 1
            a_ts[piece] = psum_bank(A_BANKS[piece % 3], [P, P * (t1 - t0)], F32, "a_t")
            for t in range(t0, t1):
                for n in range(NTAP):
                    nc.tensor.matmul(
                        out=a_ts[piece][:, P * (t - t0) : P * (t - t0 + 1)],
                        lhsT=prods[g % NPROD][:, n, t].rearrange("p b s -> p (b s)"),
                        rhs=ident_f[:],
                        is_transpose=True,
                        start=(n == 0),
                        stop=(n == NTAP - 1),
                    )

        def soft(g):
            nc.vector.tensor_reduce(out=neg_max[:, g : g + 1], in_=a_ts[g][:], axis=AX.X, op=ALU.max, negate=True)
            nc.scalar.activation(
                out=e_flat[:, PIECE_COLS[g] : PIECE_COLS[g + 1]],
                in_=a_ts[g][:],
                func=ACT.Exp,
                bias=neg_max[:, g : g + 1],
                scale=1.0,
                accum_out=part_sum[:, g : g + 1],
            )

        for g in range(N_RIGHT - 1):
            expand_right(g)
        spread(0)
        for g in range(G):
            if g + 1 < G:
                spread(g + 1)
            halves = ((0, T),) if g < G - 1 else ((0, 3), (3, T))
            for t0, t1 in halves:
                products_gpsimd(g, t0, t1)
                products_vector(g, t0, t1)
                add_taps(g, t0, t1)
            load_scales(g)
            if g >= 1:
                soft(g - 1)
            if g + N_RIGHT - 1 < G:
                expand_right(g + N_RIGHT - 1)
            if g == 2:
                bias_ps = psum_bank(BIAS_BANK, [P, P], BF16, "bias_ps")
                nc.tensor.transpose(bias_ps[:], bias_rows[:], ident_b[:])
            if g == 4:
                nc.vector.tensor_copy(out=bias_sb[:], in_=bias_ps[:, 0:32])
        soft(G - 1)
        soft(G)

        nc.vector.tensor_reduce(out=neg_max_all[:], in_=neg_max[:], axis=AX.X, op=ALU.min)
        nc.scalar.activation(out=factor[:], in_=neg_max[:], func=ACT.Exp, bias=neg_max_all[:], scale=-1.0)
        nc.vector.scalar_tensor_tensor(
            out=weighted[:], in0=factor[:], scalar=1.0, in1=part_sum[:], op0=ALU.mult, op1=ALU.mult, accum_out=total[:]
        )
        nc.vector.reciprocal(out=recip[:], in_=total[:])
        nc.vector.tensor_scalar(out=coef[:], in0=factor[:], scalar1=recip[:], scalar2=None, op0=ALU.mult)

        u_ts = {}
        accs = {}

        def back(g):
            u = work.tile([P, 512], F32, name="u", bufs=4)
            for piece in (g,) if g < G - 1 else (g, g + 1):
                c0, c1 = PIECE_COLS[piece], PIECE_COLS[piece + 1]
                nc.scalar.activation(
                    out=u[:, c0 - 512 * g : c1 - 512 * g],
                    in_=e_flat[:, c0:c1],
                    func=ACT.Copy,
                    scale=coef[:, piece : piece + 1],
                    bias=1.0,
                )
            u_t = psum_bank(U_BANKS[g % 4], [P, T, NB, 64], F32, "u_t")
            u_ts[g] = u_t
            for t in range(T):
                nc.tensor.transpose(
                    u_t[:, t].rearrange("p b s -> p (b s)"), u[:, P * t : P * (t + 1)], ident_f[:]
                )

        groupeds = {}

        def multiply(g):
            grouped = work.tile([P, NB, 64, T], BF16, name="grouped", align_bytes=64)
            groupeds[g] = grouped
            nc.vector.tensor_tensor(
                out=grouped[:],
                in0=u_ts[g][:].rearrange("p t b s -> p b s t"),
                in1=x_sb[:, :, T * g : T * (g + 1), :].rearrange("p b t s -> p b s t"),
                op=ALU.mult,
            )

        def quantise(g):
            nc.vector.quantize_mx(
                out=x1_codes[:, g, :].bitcast(FP8X4),
                scales=x1_planes[:, g, :],
                in_=groupeds[g][:].rearrange("p b s t -> p (b s t)"),
            )

        half_flat = [prods[k][:].rearrange("p n t b s -> p (n t b s)") for k in range(2)]

        def half_sum(unit):
            return half_flat[unit // 5][:, 512 * (unit % 5) : 512 * (unit % 5 + 1)].rearrange("p (k c) -> p k c", k=4)

        def mx_pass(acc, unit, k, g):
            cols = slice(P * (4 * unit + k), P * (4 * unit + k + 1))
            nc.tensor.matmul_mx(
                out=acc[:, k, :],
                lhsT=w_words[:, g, cols].bitcast(FP8X4),
                lhsT_scale=planes[g // 4][4 * (g % 4) : P, cols],
                rhs=x1_codes[:, g, :].bitcast(FP8X4),
                rhs_scale=x1_planes[:, g, :],
                start=(g % HALF == 0),
                stop=(g % HALF == HALF - 1),
            )

        def wave(g):
            for unit in range(WAVE):
                mx_pass(accs[unit], unit, 0, g)

        for unit in range(WAVE):
            accs[unit] = psum_bank(ACC_BANKS[unit], [P, 4, P], F32, "acc")
        for g in range(4):
            back(g)
        for pair in range(2):
            multiply(2 * pair)
            multiply(2 * pair + 1)
            quantise(2 * pair)
            quantise(2 * pair + 1)
            back(2 * pair + 4)
            back(2 * pair + 5)
            wave(2 * pair)
            wave(2 * pair + 1)
        for pair in range(2, 4):
            multiply(2 * pair)
            multiply(2 * pair + 1)
            quantise(2 * pair)
            quantise(2 * pair + 1)

        for unit in range(8):
            if unit >= WAVE:
                accs[unit] = psum_bank(ACC_BANKS[unit % 4], [P, 4, P], F32, "acc")
            for k in range(1 if unit < WAVE else 0, 4):
                for g in range(HALF):
                    mx_pass(accs[unit], unit, k, g)
            for k in range(4):
                nc.scalar.activation(
                    out=half_sum(unit)[:, k, :],
                    in_=accs[unit][:, k, :],
                    func=ACT.Identity,
                    bias=bias_sb[:, 4 * unit + k : 4 * unit + k + 1],
                )

        out_v = out.rearrange("b (k p) i j -> b p k (i j)", p=P)
        for unit in range(8):
            acc = psum_bank((unit + 4) % 8, [P, 4, P], F32, "acc")
            res = work.tile([P, 4, NB, 64], F32, name="res", bufs=6)
            if unit < 7:
                for k in range(4):
                    for g in range(HALF, G):
                        mx_pass(acc, unit, k, g)
                nc.vector.tensor_tensor(
                    out=res[:].rearrange("p k b s -> p k (b s)"), in0=acc[:], in1=half_sum(unit), op=ALU.add
                )
                for b in range(NB):
                    nc.sync.dma_start(out=out_v[b][:, 4 * unit : 4 * unit + 4, :], in_=res[:, :, b, :])
            else:
                for k in range(4):
                    for g in range(HALF, G):
                        mx_pass(acc, unit, k, g)
                    nc.vector.tensor_tensor(
                        out=res[:, k].rearrange("p b s -> p (b s)"),
                        in0=acc[:, k, :],
                        in1=half_sum(unit)[:, k, :],
                        op=ALU.add,
                    )
                    if k % 2 == 1:
                        for b in range(NB):
                            nc.sync.dma_start(
                                out=out_v[b][:, 4 * unit + k - 1 : 4 * unit + k + 1, :], in_=res[:, k - 1 : k + 1, b, :]
                            )
